import numpy as np
import ml_dtypes


def mxq(x, axis, fmt="e4m3"):
    dtype, down = {"e4m3": (ml_dtypes.float8_e4m3fn, 7), "e5m2": (ml_dtypes.float8_e5m2, 14)}[fmt]
    v = np.moveaxis(np.asarray(x, np.float32).astype(ml_dtypes.bfloat16).astype(np.float64), axis, -1)
    blocks = v.reshape(v.shape[:-1] + (-1, 32))
    amax = np.abs(blocks).max(-1, keepdims=True)
    byte = np.maximum(np.where(amax > 0, np.frexp(amax)[1] - 1 + 127, 0) - down, 1)
    scale = np.exp2(byte - 127.0)
    codes = (blocks / scale).astype(np.float32).astype(dtype).astype(np.float64)
    return np.moveaxis((codes * scale).reshape(v.shape), -1, axis)


WIDE = False


def mx_kscale(k):
    if not WIDE:
        return np.ones(k)
    levels = np.array([10, -10, 5, -5, 0])
    a = np.random.permutation(np.resize(levels, k // 512 * 4)).reshape(k // 512, 4)
    idx = np.arange(k)
    return np.exp2(a[idx // 512, idx % 128 // 32])


BF16 = ml_dtypes.bfloat16


def bf(x):
    return np.asarray(x, np.float32).astype(BF16)


def f64(x):
    return np.asarray(x).astype(np.float64)


T, H, I, R = 256, 1024, 3584, 512


def silu(v):
    return v / (1.0 + np.exp(-v))


def setup_inputs():
    s, t = mx_kscale(H), mx_kscale(R)
    return {
        "x": bf(np.random.standard_normal((T, H)) * s),
        "Wmean1": bf(np.random.standard_normal((I, H)) / np.sqrt(H) / s),
        "Wmean3": bf(np.random.standard_normal((I, H)) / np.sqrt(H) / s),
        "du1": bf(np.random.standard_normal((I, R)) * 0.5 / np.sqrt(R) / t),
        "dv1": bf(np.random.standard_normal((R, H)) / np.sqrt(H) / s * t[:, None]),
        "du3": bf(np.random.standard_normal((I, R)) * 0.5 / np.sqrt(R) / t),
        "dv3": bf(np.random.standard_normal((R, H)) / np.sqrt(H) / s * t[:, None]),
    }


def reference(x, Wmean1, Wmean3, du1, dv1, du3, dv3):
    xq = mxq(f64(x), 1, "e4m3")
    p3 = xq @ mxq(f64(dv3), 1, "e4m3").T
    up = (xq @ mxq(f64(Wmean3), 1, "e4m3").T) + (mxq(p3, 1, "e4m3") @ mxq(f64(du3), 1, "e4m3").T)
    p1 = xq @ mxq(f64(dv1), 1, "e4m3").T
    gate = (xq @ mxq(f64(Wmean1), 1, "e4m3").T) + (mxq(p1, 1, "e4m3") @ mxq(f64(du1), 1, "e4m3").T)
    return silu(gate) * up

@@ -1,0 +1,241 @@
+from contextlib import ExitStack
+
+import concourse.mybir as mybir
+from concourse.masks import make_identity
+
+BF16 = mybir.dt.bfloat16
+F32 = mybir.dt.float32
+U32 = mybir.dt.uint32
+U8 = mybir.dt.uint8
+FP8X4 = mybir.dt.float8_e4m3fn_x4
+
+T, H, I, R = 256, 1024, 3584, 512
+P = 128
+CHUNK = 512
+N_CHUNKS = I // CHUNK
+N_HALVES = 2 * N_CHUNKS
+T_BANKS = 6
+
+FLOPS = 2 * T * (2 * H * I + 2 * H * R + 2 * R * I)
+
+MANUAL = True
+COPY_EVEN = "svsvss"
+COPY_ODD = "ssssss"
+
+
+def tile_merge_mixtralsparsemoeblock_pa_kernel(
+    tc, x, Wmean1, Wmean3, du1, dv1, du3, dv3, out
+):
+    nc = tc.nc
+    with ExitStack() as ctx:
+        const = ctx.enter_context(tc.tile_pool(name="const", bufs=1))
+        raw = ctx.enter_context(tc.tile_pool(name="raw", bufs=12))
+        grp = ctx.enter_context(tc.tile_pool(name="grp", bufs=6))
+        cod = ctx.enter_context(tc.tile_pool(name="cod", bufs=8))
+        epi = ctx.enter_context(tc.tile_pool(name="epi", bufs=4))
+        psum = ctx.enter_context(tc.psum_pool(name="psum", bufs=1))
+        if MANUAL:
+            ctx.enter_context(tc.manual_schedule())
+
+        ident = const.tile([P, P], F32, name="ident")
+        make_identity(nc, ident[:])
+        warm = const.tile([P, 8], F32, name="warm")
+        nc.vector.memset(warm[:], 0.0)
+        nc.scalar.activation(
+            out=warm[:, 4:8], in_=warm[:, 0:4], func=mybir.ActivationFunctionType.Silu
+        )
+
+        out_v = out.rearrange("(p j) i -> j p i", j=2)
+
+        def load(tag, width, src):
+            t = raw.tile([P, width], BF16, tag=tag, name=tag)
+            nc.sync.dma_start(out=t[:], in_=src)
+            return t
+
+        def load_dv(dv):
+            t = raw.tile([P, 4096], BF16, tag="w", name="w")
+            nc.sync.dma_start(
+                out=t[:].rearrange("p (u f) -> p u f", u=2),
+                in_=dv.rearrange("(u p e) k -> p u (e k)", u=2, e=2),
+            )
+            return t
+
+        def load_chunk(c):
+            rows = slice(c * CHUNK, (c + 1) * CHUNK)
+            w1 = load("w", 4096, Wmean1[rows, :].rearrange("(p j) k -> p (j k)", j=4))
+            d1 = load("d", 2048, du1[rows, :].rearrange("(p j) k -> p (j k)", j=4))
+            w3 = load("w", 4096, Wmean3[rows, :].rearrange("(p j) k -> p (j k)", j=4))
+            d3 = load("d", 2048, du3[rows, :].rearrange("(p j) k -> p (j k)", j=4))
+            return [(w1, d1), (w3, d3)]
+
+        bank_no = [0]
+
+        def transpose_bank(words, srcs):
+            k = bank_no[0] % T_BANKS
+            bank_no[0] = bank_no[0] + 1
+            tb = psum.tile([P, 512], F32, tag="tb%d" % k, name="tb%d" % k)
+            for pos, src in enumerate(srcs):
+                nc.tensor.transpose(
+                    tb[:, pos * P : (pos + 1) * P], words[:, src : src + P], ident[:]
+                )
+            return tb
+
+        def unit_srcs(stride, g, b):
+            return [
+                (2 * b + a) * stride + g * 256 + u * P for u in range(2) for a in range(2)
+            ]
+
+        def copy_bank(engine, tb, dst_words):
+            dst = dst_words.rearrange("q (n u) -> q n u", u=2)
+            src = tb[:].rearrange("q (u n) -> q n u", u=2)
+            if engine == "s":
+                nc.scalar.copy(out=dst, in_=src)
+            else:
+                nc.vector.tensor_copy(out=dst, in_=src)
+
+        def copy_units(banks, engines):
+            groups = []
+            for i in range(len(banks) // 2):
+                g = grp.tile([P, 2048], BF16, tag="g", name="g", align_bytes=64)
+                gw = g[:].bitcast(F32)
+                for b in range(2):
+                    copy_bank(engines[2 * i + b], banks[2 * i + b], gw[:, b * 512 : (b + 1) * 512])
+                groups.append(g)
+            return groups
+
+        def quantise(pool, g, width, tag):
+            c = pool.tile([P, width // 4], U32, tag="c" + tag, name="c" + tag, align_bytes=64)
+            s = pool.tile([P, width // 4], U8, tag="s" + tag, name="s" + tag, align_bytes=64)
+            nc.vector.quantize_mx(out=c[:].bitcast(FP8X4), scales=s[:], in_=g[:])
+            return (c, s)
+
+        def mx(acc, lhs, lcols, rhs, rcols, start, stop):
+            nc.tensor.matmul_mx(
+                out=acc,
+                lhsT=lhs[0][:, lcols].bitcast(FP8X4),
+                lhsT_scale=lhs[1][:, lcols],
+                rhs=rhs[0][:, rcols].bitcast(FP8X4),
+                rhs_scale=rhs[1][:, rcols],
+                start=start,
+                stop=stop,
+            )
+
+        def t_weight(wt, dt):
+            banks = []
+            ww = wt[:].bitcast(F32)
+            for g in range(2):
+                for b in range(2):
+                    banks.append(transpose_bank(ww, unit_srcs(512, g, b)))
+            if dt is not None:
+                dw = dt[:].bitcast(F32)
+                for b in range(2):
+                    banks.append(transpose_bank(dw, unit_srcs(256, 0, b)))
+            return banks
+
+        def cq(banks, engines):
+            groups = copy_units(banks, engines)
+            return [quantise(cod, g, 2048, "u") for g in groups]
+
+        def mx_p(dvq):
+            accs = []
+            for m in range(2):
+                acc = psum.tile([P, 512], F32, tag="acc%d" % m, name="acc%d" % m)
+                for t in range(4):
+                    for g in range(2):
+                        mx(
+                            acc[:, t * P : (t + 1) * P],
+                            dvq[g],
+                            slice(t * P, (t + 1) * P),
+                            xq,
+                            slice(g * 256 + m * P, g * 256 + (m + 1) * P),
+                            g == 0,
+                            g == 1,
+                        )
+                accs.append(acc)
+            return accs
+
+        def q_p(accs, d):
+            pg = const.tile([P, 1024], BF16, name="pg%d" % d, align_bytes=64)
+            for m in range(2):
+                dst = pg[:, m * 512 : (m + 1) * 512].rearrange("q (n t) -> q n t", t=4)
+                src = accs[m][:].rearrange("q (t n) -> q n t", t=4)
+                if m == 0:
+                    nc.vector.tensor_copy(out=dst, in_=src)
+                else:
+                    nc.scalar.copy(out=dst, in_=src)
+            return pg
+
+        def mx_half(units, pq):
+            accs = []
+            for m in range(2):
+                acc = psum.tile([P, 512], F32, tag="acc%d" % m, name="acc%d" % m)
+                full = slice(0, 512)
+                mx(acc[:], xq, slice(m * P, (m + 1) * P), units[0], full, True, False)
+                mx(acc[:], xq, slice(256 + m * P, 256 + (m + 1) * P), units[1], full, False, False)
+                mx(acc[:], pq, slice(m * P, (m + 1) * P), units[2], full, False, True)
+                accs.append(acc)
+            return accs
+
+        def natural(ap):
+            return ap.rearrange("t (j p) -> t p j", j=4)
+
+        def flat(ap):
+            return ap.rearrange("t (p j) -> t p j", j=4)
+
+        x_raw = load("d", 2048, x.rearrange("(p j) k -> p (j k)", j=2))
+        dv_raw = [load_dv(dv1), load_dv(dv3)]
+        chunks = [load_chunk(c) for c in range(5)]
+
+        xw = x_raw[:].bitcast(F32)
+        x_banks = [
+            transpose_bank(xw, [a * 512 + g * 256 + u * P for u in range(2) for a in range(2)])
+            for g in range(2)
+        ]
+        xg = copy_units(x_banks, "sv")[0]
+        xq = quantise(const, xg, 2048, "x")
+
+        dvq = []
+        for d in range(2):
+            banks = t_weight(dv_raw[d], None)
+            dvq.append(cq(banks, "svsv"))
+        chunks.append(load_chunk(5))
+
+        halves = {}
+        pqs = []
+        for d in range(2):
+            p_acc = mx_p(dvq[d])
+            banks = t_weight(chunks[0][d][0], chunks[0][d][1])
+            pg = q_p(p_acc, d)
+            groups = copy_units(banks, "svsvsv")
+            pqs.append(quantise(const, pg, 1024, "p%d" % d))
+            halves[d] = [quantise(cod, g, 2048, "u") for g in groups]
+        chunks.append(load_chunk(6))
+
+        sil = {}
+        for h in range(N_HALVES):
+            c, d = divmod(h, 2)
+            accs = mx_half(halves[h], pqs[d])
+            for m in range(2):
+                if d == 0:
+                    s = epi.tile([P, 512], F32, tag="sil", name="sil")
+                    nc.scalar.activation(
+                        out=flat(s[:]),
+                        in_=natural(accs[m][:]),
+                        func=mybir.ActivationFunctionType.Silu,
+                    )
+                    sil[m] = s
+                else:
+                    o = epi.tile([P, 512], F32, tag="o", name="o")
+                    nc.vector.tensor_tensor(
+                        out=flat(o[:]),
+                        in0=natural(accs[m][:]),
+                        in1=flat(sil[m][:]),
+                        op=mybir.AluOpType.mult,
+                    )
+                    queue = nc.sync if c == N_CHUNKS - 1 else nc.gpsimd
+                    queue.dma_start(out=out_v[m][:, c * CHUNK : (c + 1) * CHUNK], in_=o[:])
+            nh = h + 2
+            if nh < N_HALVES:
+                wt, dt = chunks[nh // 2][nh % 2]
+                banks = t_weight(wt, dt)
+                halves[nh] = cq(banks, COPY_EVEN if nh % 2 == 0 else COPY_ODD)

@@ -8,19 +8,18 @@ F32 = mybir.dt.float32
 U32 = mybir.dt.uint32
 U8 = mybir.dt.uint8
 FP8X4 = mybir.dt.float8_e4m3fn_x4
+SILU = mybir.ActivationFunctionType.Silu
 
 T, H, I, R = 256, 1024, 3584, 512
 P = 128
+BANK = 512
+N_BANKS = 8
 CHUNK = 512
 N_CHUNKS = I // CHUNK
-N_HALVES = 2 * N_CHUNKS
-T_BANKS = 6
+BY_HALVES = 2
+PRELOAD = 3
 
 FLOPS = 2 * T * (2 * H * I + 2 * H * R + 2 * R * I)
-
-MANUAL = True
-COPY_EVEN = "svsvss"
-COPY_ODD = "ssssss"
 
 
 def tile_merge_mixtralsparsemoeblock_pa_kernel(
@@ -29,21 +28,19 @@ def tile_merge_mixtralsparsemoeblock_pa_kernel(
     nc = tc.nc
     with ExitStack() as ctx:
         const = ctx.enter_context(tc.tile_pool(name="const", bufs=1))
-        raw = ctx.enter_context(tc.tile_pool(name="raw", bufs=12))
-        grp = ctx.enter_context(tc.tile_pool(name="grp", bufs=6))
-        cod = ctx.enter_context(tc.tile_pool(name="cod", bufs=8))
-        epi = ctx.enter_context(tc.tile_pool(name="epi", bufs=4))
+        raw = ctx.enter_context(tc.tile_pool(name="raw", bufs=2 * PRELOAD + 2))
+        grp = ctx.enter_context(tc.tile_pool(name="grp", bufs=8))
+        cod = ctx.enter_context(tc.tile_pool(name="cod", bufs=14))
+        act = ctx.enter_context(tc.tile_pool(name="act", bufs=4))
+        res = ctx.enter_context(tc.tile_pool(name="res", bufs=2 * N_CHUNKS))
         psum = ctx.enter_context(tc.psum_pool(name="psum", bufs=1))
-        if MANUAL:
-            ctx.enter_context(tc.manual_schedule())
+        ctx.enter_context(tc.manual_schedule())
 
         ident = const.tile([P, P], F32, name="ident")
         make_identity(nc, ident[:])
         warm = const.tile([P, 8], F32, name="warm")
         nc.vector.memset(warm[:], 0.0)
-        nc.scalar.activation(
-            out=warm[:, 4:8], in_=warm[:, 0:4], func=mybir.ActivationFunctionType.Silu
-        )
+        nc.scalar.activation(out=warm[:, 4:8], in_=warm[:, 0:4], func=SILU)
 
         out_v = out.rearrange("(p j) i -> j p i", j=2)
 
@@ -60,46 +57,62 @@ def tile_merge_mixtralsparsemoeblock_pa_kernel(
             )
             return t
 
-        def load_chunk(c):
+        chunks = []
+
+        def load_next_chunk():
+            c = len(chunks)
+            if c == N_CHUNKS:
+                return
             rows = slice(c * CHUNK, (c + 1) * CHUNK)
             w1 = load("w", 4096, Wmean1[rows, :].rearrange("(p j) k -> p (j k)", j=4))
             d1 = load("d", 2048, du1[rows, :].rearrange("(p j) k -> p (j k)", j=4))
             w3 = load("w", 4096, Wmean3[rows, :].rearrange("(p j) k -> p (j k)", j=4))
             d3 = load("d", 2048, du3[rows, :].rearrange("(p j) k -> p (j k)", j=4))
-            return [(w1, d1), (w3, d3)]
+            chunks.append([(w1, d1), (w3, d3)])
 
-        bank_no = [0]
+        ring = [0]
 
-        def transpose_bank(words, srcs):
-            k = bank_no[0] % T_BANKS
-            bank_no[0] = bank_no[0] + 1
-            tb = psum.tile([P, 512], F32, tag="tb%d" % k, name="tb%d" % k)
-            for pos, src in enumerate(srcs):
-                nc.tensor.transpose(
-                    tb[:, pos * P : (pos + 1) * P], words[:, src : src + P], ident[:]
-                )
-            return tb
+        def next_bank():
+            k = ring[0] % N_BANKS
+            ring[0] = ring[0] + 1
+            return psum.tile([P, BANK], F32, tag="bank%d" % k, name="bank%d" % k)
 
-        def unit_srcs(stride, g, b):
-            return [
-                (2 * b + a) * stride + g * 256 + u * P for u in range(2) for a in range(2)
-            ]
+        def transpose_bank(words, first, stride, k0):
+            bank = next_bank()
+            for u in range(2):
+                for a in range(2):
+                    src = (first + a) * stride + k0 + u * P
+                    pos = (2 * u + a) * P
+                    nc.tensor.transpose(bank[:, pos : pos + P], words[:, src : src + P], ident[:])
+            return bank
 
-        def copy_bank(engine, tb, dst_words):
-            dst = dst_words.rearrange("q (n u) -> q n u", u=2)
-            src = tb[:].rearrange("q (u n) -> q n u", u=2)
-            if engine == "s":
-                nc.scalar.copy(out=dst, in_=src)
-            else:
+        def transpose_weight(wt, dt):
+            banks = []
+            for g in range(2):
+                for b in range(2):
+                    banks.append(transpose_bank(wt[:].bitcast(F32), 2 * b, 512, 256 * g))
+            if dt is not None:
+                for b in range(2):
+                    banks.append(transpose_bank(dt[:].bitcast(F32), 2 * b, 256, 0))
+            return banks
+
+        def copy_out(on_vector, dst, src):
+            if on_vector:
                 nc.vector.tensor_copy(out=dst, in_=src)
+            else:
+                nc.scalar.copy(out=dst, in_=src)
 
-        def copy_units(banks, engines):
+        def regroup(banks, vector_helps):
             groups = []
             for i in range(len(banks) // 2):
                 g = grp.tile([P, 2048], BF16, tag="g", name="g", align_bytes=64)
                 gw = g[:].bitcast(F32)
                 for b in range(2):
-                    copy_bank(engines[2 * i + b], banks[2 * i + b], gw[:, b * 512 : (b + 1) * 512])
+                    copy_out(
+                        vector_helps and b == 1,
+                        gw[:, b * BANK : (b + 1) * BANK].rearrange("q (n u) -> q n u", u=2),
+                        banks[2 * i + b][:].rearrange("q (u n) -> q n u", u=2),
+                    )
                 groups.append(g)
             return groups
 
@@ -109,72 +122,16 @@ def tile_merge_mixtralsparsemoeblock_pa_kernel(
             nc.vector.quantize_mx(out=c[:].bitcast(FP8X4), scales=s[:], in_=g[:])
             return (c, s)
 
-        def mx(acc, lhs, lcols, rhs, rcols, start, stop):
+        def mx(acc, lhs, l0, rhs, r0, n, start, stop):
             nc.tensor.matmul_mx(
                 out=acc,
-                lhsT=lhs[0][:, lcols].bitcast(FP8X4),
-                lhsT_scale=lhs[1][:, lcols],
-                rhs=rhs[0][:, rcols].bitcast(FP8X4),
-                rhs_scale=rhs[1][:, rcols],
+                lhsT=lhs[0][:, l0 : l0 + P].bitcast(FP8X4),
+                lhsT_scale=lhs[1][:, l0 : l0 + P],
+                rhs=rhs[0][:, r0 : r0 + n].bitcast(FP8X4),
+                rhs_scale=rhs[1][:, r0 : r0 + n],
                 start=start,
                 stop=stop,
             )
-
-        def t_weight(wt, dt):
-            banks = []
-            ww = wt[:].bitcast(F32)
-            for g in range(2):
-                for b in range(2):
-                    banks.append(transpose_bank(ww, unit_srcs(512, g, b)))
-            if dt is not None:
-                dw = dt[:].bitcast(F32)
-                for b in range(2):
-                    banks.append(transpose_bank(dw, unit_srcs(256, 0, b)))
-            return banks
-
-        def cq(banks, engines):
-            groups = copy_units(banks, engines)
-            return [quantise(cod, g, 2048, "u") for g in groups]
-
-        def mx_p(dvq):
-            accs = []
-            for m in range(2):
-                acc = psum.tile([P, 512], F32, tag="acc%d" % m, name="acc%d" % m)
-                for t in range(4):
-                    for g in range(2):
-                        mx(
-                            acc[:, t * P : (t + 1) * P],
-                            dvq[g],
-                            slice(t * P, (t + 1) * P),
-                            xq,
-                            slice(g * 256 + m * P, g * 256 + (m + 1) * P),
-                            g == 0,
-                            g == 1,
-                        )
-                accs.append(acc)
-            return accs
-
-        def q_p(accs, d):
-            pg = const.tile([P, 1024], BF16, name="pg%d" % d, align_bytes=64)
-            for m in range(2):
-                dst = pg[:, m * 512 : (m + 1) * 512].rearrange("q (n t) -> q n t", t=4)
-                src = accs[m][:].rearrange("q (t n) -> q n t", t=4)
-                if m == 0:
-                    nc.vector.tensor_copy(out=dst, in_=src)
-                else:
-                    nc.scalar.copy(out=dst, in_=src)
-            return pg
-
-        def mx_half(units, pq):
-            accs = []
-            for m in range(2):
-                acc = psum.tile([P, 512], F32, tag="acc%d" % m, name="acc%d" % m)
-                full = slice(0, 512)
-                mx(acc[:], xq, slice(m * P, (m + 1) * P), units[0], full, True, False)
-                mx(acc[:], xq, slice(256 + m * P, 256 + (m + 1) * P), units[1], full, False, False)
-                mx(acc[:], pq, slice(m * P, (m + 1) * P), units[2], full, False, True)
-                accs.append(acc)
-            return accs
 
         def natural(ap):
             return ap.rearrange("t (j p) -> t p j", j=4)
@@ -182,60 +139,105 @@ def tile_merge_mixtralsparsemoeblock_pa_kernel(
         def flat(ap):
             return ap.rearrange("t (p j) -> t p j", j=4)
 
+        small = {}
+        silu_of = {}
+
+        def transpose(item):
+            kind, arg = item
+            if kind == "x":
+                return [transpose_bank(x_raw[:].bitcast(F32), 0, 512, 256 * g) for g in range(2)]
+            if kind == "dv":
+                return transpose_weight(dv_raw[arg], None)
+            banks = []
+            for h in arg:
+                banks.extend(transpose_weight(chunks[h // 2][h % 2][0], chunks[h // 2][h % 2][1]))
+            return banks
+
+        def quantise_item(item, banks):
+            kind, arg = item
+            if kind == "x":
+                small["x"] = quantise(const, regroup(banks, True)[0], 2048, "x")
+                return None
+            if kind == "dv":
+                groups = regroup(banks, True)
+            else:
+                groups = []
+                for i, h in enumerate(arg):
+                    groups.extend(regroup(banks[6 * i : 6 * i + 6], h % 2 == 0))
+            return [quantise(cod, g, 2048, "u") for g in groups]
+
+        def multiply(item, units):
+            kind, arg = item
+            accs = []
+            if kind == "dv":
+                for m in range(2):
+                    acc = next_bank()
+                    for t in range(4):
+                        for g in range(2):
+                            mx(acc[:, t * P : (t + 1) * P], units[g], t * P,
+                               small["x"], 256 * g + m * P, P, g == 0, g == 1)
+                    accs.append(acc)
+            if kind == "w":
+                for i, h in enumerate(arg):
+                    for m in range(2):
+                        acc = next_bank()
+                        mx(acc[:], small["x"], m * P, units[3 * i], 0, BANK, True, False)
+                        mx(acc[:], small["x"], 256 + m * P, units[3 * i + 1], 0, BANK, False, False)
+                        mx(acc[:], small[h % 2], m * P, units[3 * i + 2], 0, BANK, False, True)
+                        accs.append(acc)
+            return accs
+
+        def finish(item, accs):
+            kind, arg = item
+            if kind == "dv":
+                pg = const.tile([P, 1024], BF16, name="pg%d" % arg, align_bytes=64)
+                for m in range(2):
+                    copy_out(
+                        m == 0,
+                        pg[:, m * 512 : (m + 1) * 512].rearrange("q (n t) -> q n t", t=4),
+                        accs[m][:].rearrange("q (t n) -> q n t", t=4),
+                    )
+                small[arg] = quantise(const, pg, 1024, "p%d" % arg)
+            if kind == "w":
+                for i, h in enumerate(arg):
+                    for m in range(2):
+                        acc = accs[2 * i + m]
+                        if h % 2 == 0:
+                            s = act.tile([P, CHUNK], F32, tag="silu", name="silu")
+                            nc.scalar.activation(out=flat(s[:]), in_=natural(acc[:]), func=SILU)
+                            silu_of[m] = s
+                        else:
+                            c = h // 2
+                            o = res.tile([P, CHUNK], F32, tag="o", name="o")
+                            nc.vector.tensor_tensor(
+                                out=flat(o[:]),
+                                in0=natural(acc[:]),
+                                in1=flat(silu_of[m][:]),
+                                op=mybir.AluOpType.mult,
+                            )
+                            nc.sync.dma_start(out=out_v[m][:, c * CHUNK : (c + 1) * CHUNK], in_=o[:])
+
         x_raw = load("d", 2048, x.rearrange("(p j) k -> p (j k)", j=2))
         dv_raw = [load_dv(dv1), load_dv(dv3)]
-        chunks = [load_chunk(c) for c in range(5)]
+        for c in range(PRELOAD):
+            load_next_chunk()
 
-        xw = x_raw[:].bitcast(F32)
-        x_banks = [
-            transpose_bank(xw, [a * 512 + g * 256 + u * P for u in range(2) for a in range(2)])
-            for g in range(2)
-        ]
-        xg = copy_units(x_banks, "sv")[0]
-        xq = quantise(const, xg, 2048, "x")
+        work = [("x", None), ("dv", 0), ("dv", 1)]
+        work.extend([("w", [h]) for h in range(2 * BY_HALVES)])
+        work.extend([("w", [2 * c, 2 * c + 1]) for c in range(BY_HALVES, N_CHUNKS)])
 
-        dvq = []
-        for d in range(2):
-            banks = t_weight(dv_raw[d], None)
-            dvq.append(cq(banks, "svsv"))
-        chunks.append(load_chunk(5))
-
-        halves = {}
-        pqs = []
-        for d in range(2):
-            p_acc = mx_p(dvq[d])
-            banks = t_weight(chunks[0][d][0], chunks[0][d][1])
-            pg = q_p(p_acc, d)
-            groups = copy_units(banks, "svsvsv")
-            pqs.append(quantise(const, pg, 1024, "p%d" % d))
-            halves[d] = [quantise(cod, g, 2048, "u") for g in groups]
-        chunks.append(load_chunk(6))
-
-        sil = {}
-        for h in range(N_HALVES):
-            c, d = divmod(h, 2)
-            accs = mx_half(halves[h], pqs[d])
-            for m in range(2):
-                if d == 0:
-                    s = epi.tile([P, 512], F32, tag="sil", name="sil")
-                    nc.scalar.activation(
-                        out=flat(s[:]),
-                        in_=natural(accs[m][:]),
-                        func=mybir.ActivationFunctionType.Silu,
-                    )
-                    sil[m] = s
-                else:
-                    o = epi.tile([P, 512], F32, tag="o", name="o")
-                    nc.vector.tensor_tensor(
-                        out=flat(o[:]),
-                        in0=natural(accs[m][:]),
-                        in1=flat(sil[m][:]),
-                        op=mybir.AluOpType.mult,
-                    )
-                    queue = nc.sync if c == N_CHUNKS - 1 else nc.gpsimd
-                    queue.dma_start(out=out_v[m][:, c * CHUNK : (c + 1) * CHUNK], in_=o[:])
-            nh = h + 2
-            if nh < N_HALVES:
-                wt, dt = chunks[nh // 2][nh % 2]
-                banks = t_weight(wt, dt)
-                halves[nh] = cq(banks, COPY_EVEN if nh % 2 == 0 else COPY_ODD)
+        units = None
+        for i in range(len(work) + 1):
+            banks = None
+            if i < len(work):
+                banks = transpose(work[i])
+                kind, arg = work[i]
+                if (kind == "dv" and arg == 1) or (kind == "w" and arg[-1] % 2 == 1):
+                    load_next_chunk()
+            accs = None
+            if i > 0:
+                accs = multiply(work[i - 1], units)
+            if i < len(work):
+                units = quantise_item(work[i], banks)
+            if i > 0:
+                finish(work[i - 1], accs)

@@ -8,18 +8,19 @@ F32 = mybir.dt.float32
 U32 = mybir.dt.uint32
 U8 = mybir.dt.uint8
 FP8X4 = mybir.dt.float8_e4m3fn_x4
-SILU = mybir.ActivationFunctionType.Silu
 
 T, H, I, R = 256, 1024, 3584, 512
 P = 128
-BANK = 512
-N_BANKS = 8
 CHUNK = 512
 N_CHUNKS = I // CHUNK
-BY_HALVES = 2
-PRELOAD = 3
+N_HALVES = 2 * N_CHUNKS
+T_BANKS = 6
 
 FLOPS = 2 * T * (2 * H * I + 2 * H * R + 2 * R * I)
+
+MANUAL = False
+COPY_EVEN = "svsvss"
+COPY_ODD = "ssssss"
 
 
 def tile_merge_mixtralsparsemoeblock_pa_kernel(
@@ -28,19 +29,21 @@ def tile_merge_mixtralsparsemoeblock_pa_kernel(
     nc = tc.nc
     with ExitStack() as ctx:
         const = ctx.enter_context(tc.tile_pool(name="const", bufs=1))
-        raw = ctx.enter_context(tc.tile_pool(name="raw", bufs=2 * PRELOAD + 2))
-        grp = ctx.enter_context(tc.tile_pool(name="grp", bufs=8))
-        cod = ctx.enter_context(tc.tile_pool(name="cod", bufs=14))
-        act = ctx.enter_context(tc.tile_pool(name="act", bufs=4))
-        res = ctx.enter_context(tc.tile_pool(name="res", bufs=2 * N_CHUNKS))
+        raw = ctx.enter_context(tc.tile_pool(name="raw", bufs=12))
+        grp = ctx.enter_context(tc.tile_pool(name="grp", bufs=6))
+        cod = ctx.enter_context(tc.tile_pool(name="cod", bufs=8))
+        epi = ctx.enter_context(tc.tile_pool(name="epi", bufs=4))
         psum = ctx.enter_context(tc.psum_pool(name="psum", bufs=1))
-        ctx.enter_context(tc.manual_schedule())
+        if MANUAL:
+            ctx.enter_context(tc.manual_schedule())
 
         ident = const.tile([P, P], F32, name="ident")
         make_identity(nc, ident[:])
         warm = const.tile([P, 8], F32, name="warm")
         nc.vector.memset(warm[:], 0.0)
-        nc.scalar.activation(out=warm[:, 4:8], in_=warm[:, 0:4], func=SILU)
+        nc.scalar.activation(
+            out=warm[:, 4:8], in_=warm[:, 0:4], func=mybir.ActivationFunctionType.Silu
+        )
 
         out_v = out.rearrange("(p j) i -> j p i", j=2)
 
@@ -57,62 +60,46 @@ def tile_merge_mixtralsparsemoeblock_pa_kernel(
             )
             return t
 
-        chunks = []
-
-        def load_next_chunk():
-            c = len(chunks)
-            if c == N_CHUNKS:
-                return
+        def load_chunk(c):
             rows = slice(c * CHUNK, (c + 1) * CHUNK)
             w1 = load("w", 4096, Wmean1[rows, :].rearrange("(p j) k -> p (j k)", j=4))
             d1 = load("d", 2048, du1[rows, :].rearrange("(p j) k -> p (j k)", j=4))
             w3 = load("w", 4096, Wmean3[rows, :].rearrange("(p j) k -> p (j k)", j=4))
             d3 = load("d", 2048, du3[rows, :].rearrange("(p j) k -> p (j k)", j=4))
-            chunks.append([(w1, d1), (w3, d3)])
+            return [(w1, d1), (w3, d3)]
 
-        ring = [0]
+        bank_no = [0]
 
-        def next_bank():
-            k = ring[0] % N_BANKS
-            ring[0] = ring[0] + 1
-            return psum.tile([P, BANK], F32, tag="bank%d" % k, name="bank%d" % k)
+        def transpose_bank(words, srcs):
+            k = bank_no[0] % T_BANKS
+            bank_no[0] = bank_no[0] + 1
+            tb = psum.tile([P, 512], F32, tag="tb%d" % k, name="tb%d" % k)
+            for pos, src in enumerate(srcs):
+                nc.tensor.transpose(
+                    tb[:, pos * P : (pos + 1) * P], words[:, src : src + P], ident[:]
+                )
+            return tb
 
-        def transpose_bank(words, first, stride, k0):
-            bank = next_bank()
-            for u in range(2):
-                for a in range(2):
-                    src = (first + a) * stride + k0 + u * P
-                    pos = (2 * u + a) * P
-                    nc.tensor.transpose(bank[:, pos : pos + P], words[:, src : src + P], ident[:])
-            return bank
+        def unit_srcs(stride, g, b):
+            return [
+                (2 * b + a) * stride + g * 256 + u * P for u in range(2) for a in range(2)
+            ]
 
-        def transpose_weight(wt, dt):
-            banks = []
-            for g in range(2):
-                for b in range(2):
-                    banks.append(transpose_bank(wt[:].bitcast(F32), 2 * b, 512, 256 * g))
-            if dt is not None:
-                for b in range(2):
-                    banks.append(transpose_bank(dt[:].bitcast(F32), 2 * b, 256, 0))
-            return banks
-
-        def copy_out(on_vector, dst, src):
-            if on_vector:
-                nc.vector.tensor_copy(out=dst, in_=src)
-            else:
+        def copy_bank(engine, tb, dst_words):
+            dst = dst_words.rearrange("q (n u) -> q n u", u=2)
+            src = tb[:].rearrange("q (u n) -> q n u", u=2)
+            if engine == "s":
                 nc.scalar.copy(out=dst, in_=src)
+            else:
+                nc.vector.tensor_copy(out=dst, in_=src)
 
-        def regroup(banks, vector_helps):
+        def copy_units(banks, engines):
             groups = []
             for i in range(len(banks) // 2):
                 g = grp.tile([P, 2048], BF16, tag="g", name="g", align_bytes=64)
                 gw = g[:].bitcast(F32)
                 for b in range(2):
-                    copy_out(
-                        vector_helps and b == 1,
-                        gw[:, b * BANK : (b + 1) * BANK].rearrange("q (n u) -> q n u", u=2),
-                        banks[2 * i + b][:].rearrange("q (u n) -> q n u", u=2),
-                    )
+                    copy_bank(engines[2 * i + b], banks[2 * i + b], gw[:, b * 512 : (b + 1) * 512])
                 groups.append(g)
             return groups
 
@@ -122,16 +109,72 @@ def tile_merge_mixtralsparsemoeblock_pa_kernel(
             nc.vector.quantize_mx(out=c[:].bitcast(FP8X4), scales=s[:], in_=g[:])
             return (c, s)
 
-        def mx(acc, lhs, l0, rhs, r0, n, start, stop):
+        def mx(acc, lhs, lcols, rhs, rcols, start, stop):
             nc.tensor.matmul_mx(
                 out=acc,
-                lhsT=lhs[0][:, l0 : l0 + P].bitcast(FP8X4),
-                lhsT_scale=lhs[1][:, l0 : l0 + P],
-                rhs=rhs[0][:, r0 : r0 + n].bitcast(FP8X4),
-                rhs_scale=rhs[1][:, r0 : r0 + n],
+                lhsT=lhs[0][:, lcols].bitcast(FP8X4),
+                lhsT_scale=lhs[1][:, lcols],
+                rhs=rhs[0][:, rcols].bitcast(FP8X4),
+                rhs_scale=rhs[1][:, rcols],
                 start=start,
                 stop=stop,
             )
+
+        def t_weight(wt, dt):
+            banks = []
+            ww = wt[:].bitcast(F32)
+            for g in range(2):
+                for b in range(2):
+                    banks.append(transpose_bank(ww, unit_srcs(512, g, b)))
+            if dt is not None:
+                dw = dt[:].bitcast(F32)
+                for b in range(2):
+                    banks.append(transpose_bank(dw, unit_srcs(256, 0, b)))
+            return banks
+
+        def cq(banks, engines):
+            groups = copy_units(banks, engines)
+            return [quantise(cod, g, 2048, "u") for g in groups]
+
+        def mx_p(dvq):
+            accs = []
+            for m in range(2):
+                acc = psum.tile([P, 512], F32, tag="acc%d" % m, name="acc%d" % m)
+                for t in range(4):
+                    for g in range(2):
+                        mx(
+                            acc[:, t * P : (t + 1) * P],
+                            dvq[g],
+                            slice(t * P, (t + 1) * P),
+                            xq,
+                            slice(g * 256 + m * P, g * 256 + (m + 1) * P),
+                            g == 0,
+                            g == 1,
+                        )
+                accs.append(acc)
+            return accs
+
+        def q_p(accs, d):
+            pg = const.tile([P, 1024], BF16, name="pg%d" % d, align_bytes=64)
+            for m in range(2):
+                dst = pg[:, m * 512 : (m + 1) * 512].rearrange("q (n t) -> q n t", t=4)
+                src = accs[m][:].rearrange("q (t n) -> q n t", t=4)
+                if m == 0:
+                    nc.vector.tensor_copy(out=dst, in_=src)
+                else:
+                    nc.scalar.copy(out=dst, in_=src)
+            return pg
+
+        def mx_half(units, pq):
+            accs = []
+            for m in range(2):
+                acc = psum.tile([P, 512], F32, tag="acc%d" % m, name="acc%d" % m)
+                full = slice(0, 512)
+                mx(acc[:], xq, slice(m * P, (m + 1) * P), units[0], full, True, False)
+                mx(acc[:], xq, slice(256 + m * P, 256 + (m + 1) * P), units[1], full, False, False)
+                mx(acc[:], pq, slice(m * P, (m + 1) * P), units[2], full, False, True)
+                accs.append(acc)
+            return accs
 
         def natural(ap):
             return ap.rearrange("t (j p) -> t p j", j=4)
@@ -139,105 +182,60 @@ def tile_merge_mixtralsparsemoeblock_pa_kernel(
         def flat(ap):
             return ap.rearrange("t (p j) -> t p j", j=4)
 
-        small = {}
-        silu_of = {}
-
-        def transpose(item):
-            kind, arg = item
-            if kind == "x":
-                return [transpose_bank(x_raw[:].bitcast(F32), 0, 512, 256 * g) for g in range(2)]
-            if kind == "dv":
-                return transpose_weight(dv_raw[arg], None)
-            banks = []
-            for h in arg:
-                banks.extend(transpose_weight(chunks[h // 2][h % 2][0], chunks[h // 2][h % 2][1]))
-            return banks
-
-        def quantise_item(item, banks):
-            kind, arg = item
-            if kind == "x":
-                small["x"] = quantise(const, regroup(banks, True)[0], 2048, "x")
-                return None
-            if kind == "dv":
-                groups = regroup(banks, True)
-            else:
-                groups = []
-                for i, h in enumerate(arg):
-                    groups.extend(regroup(banks[6 * i : 6 * i + 6], h % 2 == 0))
-            return [quantise(cod, g, 2048, "u") for g in groups]
-
-        def multiply(item, units):
-            kind, arg = item
-            accs = []
-            if kind == "dv":
-                for m in range(2):
-                    acc = next_bank()
-                    for t in range(4):
-                        for g in range(2):
-                            mx(acc[:, t * P : (t + 1) * P], units[g], t * P,
-                               small["x"], 256 * g + m * P, P, g == 0, g == 1)
-                    accs.append(acc)
-            if kind == "w":
-                for i, h in enumerate(arg):
-                    for m in range(2):
-                        acc = next_bank()
-                        mx(acc[:], small["x"], m * P, units[3 * i], 0, BANK, True, False)
-                        mx(acc[:], small["x"], 256 + m * P, units[3 * i + 1], 0, BANK, False, False)
-                        mx(acc[:], small[h % 2], m * P, units[3 * i + 2], 0, BANK, False, True)
-                        accs.append(acc)
-            return accs
-
-        def finish(item, accs):
-            kind, arg = item
-            if kind == "dv":
-                pg = const.tile([P, 1024], BF16, name="pg%d" % arg, align_bytes=64)
-                for m in range(2):
-                    copy_out(
-                        m == 0,
-                        pg[:, m * 512 : (m + 1) * 512].rearrange("q (n t) -> q n t", t=4),
-                        accs[m][:].rearrange("q (t n) -> q n t", t=4),
-                    )
-                small[arg] = quantise(const, pg, 1024, "p%d" % arg)
-            if kind == "w":
-                for i, h in enumerate(arg):
-                    for m in range(2):
-                        acc = accs[2 * i + m]
-                        if h % 2 == 0:
-                            s = act.tile([P, CHUNK], F32, tag="silu", name="silu")
-                            nc.scalar.activation(out=flat(s[:]), in_=natural(acc[:]), func=SILU)
-                            silu_of[m] = s
-                        else:
-                            c = h // 2
-                            o = res.tile([P, CHUNK], F32, tag="o", name="o")
-                            nc.vector.tensor_tensor(
-                                out=flat(o[:]),
-                                in0=natural(acc[:]),
-                                in1=flat(silu_of[m][:]),
-                                op=mybir.AluOpType.mult,
-                            )
-                            nc.sync.dma_start(out=out_v[m][:, c * CHUNK : (c + 1) * CHUNK], in_=o[:])
-
         x_raw = load("d", 2048, x.rearrange("(p j) k -> p (j k)", j=2))
         dv_raw = [load_dv(dv1), load_dv(dv3)]
-        for c in range(PRELOAD):
-            load_next_chunk()
+        chunks = [load_chunk(c) for c in range(5)]
 
-        work = [("x", None), ("dv", 0), ("dv", 1)]
-        work.extend([("w", [h]) for h in range(2 * BY_HALVES)])
-        work.extend([("w", [2 * c, 2 * c + 1]) for c in range(BY_HALVES, N_CHUNKS)])
+        xw = x_raw[:].bitcast(F32)
+        x_banks = [
+            transpose_bank(xw, [a * 512 + g * 256 + u * P for u in range(2) for a in range(2)])
+            for g in range(2)
+        ]
+        xg = copy_units(x_banks, "sv")[0]
+        xq = quantise(const, xg, 2048, "x")
 
-        units = None
-        for i in range(len(work) + 1):
-            banks = None
-            if i < len(work):
-                banks = transpose(work[i])
-                kind, arg = work[i]
-                if (kind == "dv" and arg == 1) or (kind == "w" and arg[-1] % 2 == 1):
-                    load_next_chunk()
-            accs = None
-            if i > 0:
-                accs = multiply(work[i - 1], units)
-            if i < len(work):
-                units = quantise_item(work[i], banks)
-            if i > 0:
-                finish(work[i - 1], accs)
+        dvq = []
+        for d in range(2):
+            banks = t_weight(dv_raw[d], None)
+            dvq.append(cq(banks, "svsv"))
+        chunks.append(load_chunk(5))
+
+        halves = {}
+        pqs = []
+        for d in range(2):
+            p_acc = mx_p(dvq[d])
+            banks = t_weight(chunks[0][d][0], chunks[0][d][1])
+            pg = q_p(p_acc, d)
+            groups = copy_units(banks, "svsvsv")
+            pqs.append(quantise(const, pg, 1024, "p%d" % d))
+            halves[d] = [quantise(cod, g, 2048, "u") for g in groups]
+        chunks.append(load_chunk(6))
+
+        sil = {}
+        for h in range(N_HALVES):
+            c, d = divmod(h, 2)
+            accs = mx_half(halves[h], pqs[d])
+            for m in range(2):
+                if d == 0:
+                    s = epi.tile([P, 512], F32, tag="sil", name="sil")
+                    nc.scalar.activation(
+                        out=flat(s[:]),
+                        in_=natural(accs[m][:]),
+                        func=mybir.ActivationFunctionType.Silu,
+                    )
+                    sil[m] = s
+                else:
+                    o = epi.tile([P, 512], F32, tag="o", name="o")
+                    nc.vector.tensor_tensor(
+                        out=flat(o[:]),
+                        in0=natural(accs[m][:]),
+                        in1=flat(sil[m][:]),
+                        op=mybir.AluOpType.mult,
+                    )
+                    queue = nc.sync if c == N_CHUNKS - 1 else nc.gpsimd
+                    queue.dma_start(out=out_v[m][:, c * CHUNK : (c + 1) * CHUNK], in_=o[:])
+            nh = h + 2
+            if nh < N_HALVES:
+                wt, dt = chunks[nh // 2][nh % 2]
+                banks = t_weight(wt, dt)
+                halves[nh] = cq(banks, COPY_EVEN if nh % 2 == 0 else COPY_ODD)

@@ -8,19 +8,18 @@ F32 = mybir.dt.float32
 U32 = mybir.dt.uint32
 U8 = mybir.dt.uint8
 FP8X4 = mybir.dt.float8_e4m3fn_x4
+SILU = mybir.ActivationFunctionType.Silu
 
 T, H, I, R = 256, 1024, 3584, 512
 P = 128
+BANK = 512
+N_BANKS = 8
 CHUNK = 512
 N_CHUNKS = I // CHUNK
-N_HALVES = 2 * N_CHUNKS
-T_BANKS = 6
+BY_HALVES = 7
+PRELOAD = 3
 
 FLOPS = 2 * T * (2 * H * I + 2 * H * R + 2 * R * I)
-
-MANUAL = False
-COPY_EVEN = "svsvss"
-COPY_ODD = "ssssss"
 
 
 def tile_merge_mixtralsparsemoeblock_pa_kernel(
@@ -29,21 +28,19 @@ def tile_merge_mixtralsparsemoeblock_pa_kernel(
     nc = tc.nc
     with ExitStack() as ctx:
         const = ctx.enter_context(tc.tile_pool(name="const", bufs=1))
-        raw = ctx.enter_context(tc.tile_pool(name="raw", bufs=12))
-        grp = ctx.enter_context(tc.tile_pool(name="grp", bufs=6))
-        cod = ctx.enter_context(tc.tile_pool(name="cod", bufs=8))
-        epi = ctx.enter_context(tc.tile_pool(name="epi", bufs=4))
+        raw = ctx.enter_context(tc.tile_pool(name="raw", bufs=2 * PRELOAD + 2))
+        grp = ctx.enter_context(tc.tile_pool(name="grp", bufs=8))
+        cod = ctx.enter_context(tc.tile_pool(name="cod", bufs=14))
+        act = ctx.enter_context(tc.tile_pool(name="act", bufs=4))
+        res = ctx.enter_context(tc.tile_pool(name="res", bufs=2 * N_CHUNKS))
         psum = ctx.enter_context(tc.psum_pool(name="psum", bufs=1))
-        if MANUAL:
-            ctx.enter_context(tc.manual_schedule())
+        ctx.enter_context(tc.manual_schedule())
 
         ident = const.tile([P, P], F32, name="ident")
         make_identity(nc, ident[:])
         warm = const.tile([P, 8], F32, name="warm")
         nc.vector.memset(warm[:], 0.0)
-        nc.scalar.activation(
-            out=warm[:, 4:8], in_=warm[:, 0:4], func=mybir.ActivationFunctionType.Silu
-        )
+        nc.scalar.activation(out=warm[:, 4:8], in_=warm[:, 0:4], func=SILU)
 
         out_v = out.rearrange("(p j) i -> j p i", j=2)
 
@@ -60,46 +57,62 @@ def tile_merge_mixtralsparsemoeblock_pa_kernel(
             )
             return t
 
-        def load_chunk(c):
+        chunks = []
+
+        def load_next_chunk():
+            c = len(chunks)
+            if c == N_CHUNKS:
+                return
             rows = slice(c * CHUNK, (c + 1) * CHUNK)
             w1 = load("w", 4096, Wmean1[rows, :].rearrange("(p j) k -> p (j k)", j=4))
             d1 = load("d", 2048, du1[rows, :].rearrange("(p j) k -> p (j k)", j=4))
             w3 = load("w", 4096, Wmean3[rows, :].rearrange("(p j) k -> p (j k)", j=4))
             d3 = load("d", 2048, du3[rows, :].rearrange("(p j) k -> p (j k)", j=4))
-            return [(w1, d1), (w3, d3)]
+            chunks.append([(w1, d1), (w3, d3)])
 
-        bank_no = [0]
+        ring = [0]
 
-        def transpose_bank(words, srcs):
-            k = bank_no[0] % T_BANKS
-            bank_no[0] = bank_no[0] + 1
-            tb = psum.tile([P, 512], F32, tag="tb%d" % k, name="tb%d" % k)
-            for pos, src in enumerate(srcs):
-                nc.tensor.transpose(
-                    tb[:, pos * P : (pos + 1) * P], words[:, src : src + P], ident[:]
-                )
-            return tb
+        def next_bank():
+            k = ring[0] % N_BANKS
+            ring[0] = ring[0] + 1
+            return psum.tile([P, BANK], F32, tag="bank%d" % k, name="bank%d" % k)
 
-        def unit_srcs(stride, g, b):
-            return [
-                (2 * b + a) * stride + g * 256 + u * P for u in range(2) for a in range(2)
-            ]
+        def transpose_bank(words, first, stride, k0):
+            bank = next_bank()
+            for u in range(2):
+                for a in range(2):
+                    src = (first + a) * stride + k0 + u * P
+                    pos = (2 * u + a) * P
+                    nc.tensor.transpose(bank[:, pos : pos + P], words[:, src : src + P], ident[:])
+            return bank
 
-        def copy_bank(engine, tb, dst_words):
-            dst = dst_words.rearrange("q (n u) -> q n u", u=2)
-            src = tb[:].rearrange("q (u n) -> q n u", u=2)
-            if engine == "s":
-                nc.scalar.copy(out=dst, in_=src)
-            else:
+        def transpose_weight(wt, dt):
+            banks = []
+            for g in range(2):
+                for b in range(2):
+                    banks.append(transpose_bank(wt[:].bitcast(F32), 2 * b, 512, 256 * g))
+            if dt is not None:
+                for b in range(2):
+                    banks.append(transpose_bank(dt[:].bitcast(F32), 2 * b, 256, 0))
+            return banks
+
+        def copy_out(on_vector, dst, src):
+            if on_vector:
                 nc.vector.tensor_copy(out=dst, in_=src)
+            else:
+                nc.scalar.copy(out=dst, in_=src)
 
-        def copy_units(banks, engines):
+        def regroup(banks, vector_helps):
             groups = []
             for i in range(len(banks) // 2):
                 g = grp.tile([P, 2048], BF16, tag="g", name="g", align_bytes=64)
                 gw = g[:].bitcast(F32)
                 for b in range(2):
-                    copy_bank(engines[2 * i + b], banks[2 * i + b], gw[:, b * 512 : (b + 1) * 512])
+                    copy_out(
+                        vector_helps and b == 1,
+                        gw[:, b * BANK : (b + 1) * BANK].rearrange("q (n u) -> q n u", u=2),
+                        banks[2 * i + b][:].rearrange("q (u n) -> q n u", u=2),
+                    )
                 groups.append(g)
             return groups
 
@@ -109,72 +122,16 @@ def tile_merge_mixtralsparsemoeblock_pa_kernel(
             nc.vector.quantize_mx(out=c[:].bitcast(FP8X4), scales=s[:], in_=g[:])
             return (c, s)
 
-        def mx(acc, lhs, lcols, rhs, rcols, start, stop):
+        def mx(acc, lhs, l0, rhs, r0, n, start, stop):
             nc.tensor.matmul_mx(
                 out=acc,
-                lhsT=lhs[0][:, lcols].bitcast(FP8X4),
-                lhsT_scale=lhs[1][:, lcols],
-                rhs=rhs[0][:, rcols].bitcast(FP8X4),
-                rhs_scale=rhs[1][:, rcols],
+                lhsT=lhs[0][:, l0 : l0 + P].bitcast(FP8X4),
+                lhsT_scale=lhs[1][:, l0 : l0 + P],
+                rhs=rhs[0][:, r0 : r0 + n].bitcast(FP8X4),
+                rhs_scale=rhs[1][:, r0 : r0 + n],
                 start=start,
                 stop=stop,
             )
-
-        def t_weight(wt, dt):
-            banks = []
-            ww = wt[:].bitcast(F32)
-            for g in range(2):
-                for b in range(2):
-                    banks.append(transpose_bank(ww, unit_srcs(512, g, b)))
-            if dt is not None:
-                dw = dt[:].bitcast(F32)
-                for b in range(2):
-                    banks.append(transpose_bank(dw, unit_srcs(256, 0, b)))
-            return banks
-
-        def cq(banks, engines):
-            groups = copy_units(banks, engines)
-            return [quantise(cod, g, 2048, "u") for g in groups]
-
-        def mx_p(dvq):
-            accs = []
-            for m in range(2):
-                acc = psum.tile([P, 512], F32, tag="acc%d" % m, name="acc%d" % m)
-                for t in range(4):
-                    for g in range(2):
-                        mx(
-                            acc[:, t * P : (t + 1) * P],
-                            dvq[g],
-                            slice(t * P, (t + 1) * P),
-                            xq,
-                            slice(g * 256 + m * P, g * 256 + (m + 1) * P),
-                            g == 0,
-                            g == 1,
-                        )
-                accs.append(acc)
-            return accs
-
-        def q_p(accs, d):
-            pg = const.tile([P, 1024], BF16, name="pg%d" % d, align_bytes=64)
-            for m in range(2):
-                dst = pg[:, m * 512 : (m + 1) * 512].rearrange("q (n t) -> q n t", t=4)
-                src = accs[m][:].rearrange("q (t n) -> q n t", t=4)
-                if m == 0:
-                    nc.vector.tensor_copy(out=dst, in_=src)
-                else:
-                    nc.scalar.copy(out=dst, in_=src)
-            return pg
-
-        def mx_half(units, pq):
-            accs = []
-            for m in range(2):
-                acc = psum.tile([P, 512], F32, tag="acc%d" % m, name="acc%d" % m)
-                full = slice(0, 512)
-                mx(acc[:], xq, slice(m * P, (m + 1) * P), units[0], full, True, False)
-                mx(acc[:], xq, slice(256 + m * P, 256 + (m + 1) * P), units[1], full, False, False)
-                mx(acc[:], pq, slice(m * P, (m + 1) * P), units[2], full, False, True)
-                accs.append(acc)
-            return accs
 
         def natural(ap):
             return ap.rearrange("t (j p) -> t p j", j=4)
@@ -182,60 +139,105 @@ def tile_merge_mixtralsparsemoeblock_pa_kernel(
         def flat(ap):
             return ap.rearrange("t (p j) -> t p j", j=4)
 
+        small = {}
+        silu_of = {}
+
+        def transpose(item):
+            kind, arg = item
+            if kind == "x":
+                return [transpose_bank(x_raw[:].bitcast(F32), 0, 512, 256 * g) for g in range(2)]
+            if kind == "dv":
+                return transpose_weight(dv_raw[arg], None)
+            banks = []
+            for h in arg:
+                banks.extend(transpose_weight(chunks[h // 2][h % 2][0], chunks[h // 2][h % 2][1]))
+            return banks
+
+        def quantise_item(item, banks):
+            kind, arg = item
+            if kind == "x":
+                small["x"] = quantise(const, regroup(banks, True)[0], 2048, "x")
+                return None
+            if kind == "dv":
+                groups = regroup(banks, True)
+            else:
+                groups = []
+                for i, h in enumerate(arg):
+                    groups.extend(regroup(banks[6 * i : 6 * i + 6], h % 2 == 0))
+            return [quantise(cod, g, 2048, "u") for g in groups]
+
+        def multiply(item, units):
+            kind, arg = item
+            accs = []
+            if kind == "dv":
+                for m in range(2):
+                    acc = next_bank()
+                    for t in range(4):
+                        for g in range(2):
+                            mx(acc[:, t * P : (t + 1) * P], units[g], t * P,
+                               small["x"], 256 * g + m * P, P, g == 0, g == 1)
+                    accs.append(acc)
+            if kind == "w":
+                for i, h in enumerate(arg):
+                    for m in range(2):
+                        acc = next_bank()
+                        mx(acc[:], small["x"], m * P, units[3 * i], 0, BANK, True, False)
+                        mx(acc[:], small["x"], 256 + m * P, units[3 * i + 1], 0, BANK, False, False)
+                        mx(acc[:], small[h % 2], m * P, units[3 * i + 2], 0, BANK, False, True)
+                        accs.append(acc)
+            return accs
+
+        def finish(item, accs):
+            kind, arg = item
+            if kind == "dv":
+                pg = const.tile([P, 1024], BF16, name="pg%d" % arg, align_bytes=64)
+                for m in range(2):
+                    copy_out(
+                        m == 0,
+                        pg[:, m * 512 : (m + 1) * 512].rearrange("q (n t) -> q n t", t=4),
+                        accs[m][:].rearrange("q (t n) -> q n t", t=4),
+                    )
+                small[arg] = quantise(const, pg, 1024, "p%d" % arg)
+            if kind == "w":
+                for i, h in enumerate(arg):
+                    for m in range(2):
+                        acc = accs[2 * i + m]
+                        if h % 2 == 0:
+                            s = act.tile([P, CHUNK], F32, tag="silu", name="silu")
+                            nc.scalar.activation(out=flat(s[:]), in_=natural(acc[:]), func=SILU)
+                            silu_of[m] = s
+                        else:
+                            c = h // 2
+                            o = res.tile([P, CHUNK], F32, tag="o", name="o")
+                            nc.vector.tensor_tensor(
+                                out=flat(o[:]),
+                                in0=natural(acc[:]),
+                                in1=flat(silu_of[m][:]),
+                                op=mybir.AluOpType.mult,
+                            )
+                            nc.sync.dma_start(out=out_v[m][:, c * CHUNK : (c + 1) * CHUNK], in_=o[:])
+
         x_raw = load("d", 2048, x.rearrange("(p j) k -> p (j k)", j=2))
         dv_raw = [load_dv(dv1), load_dv(dv3)]
-        chunks = [load_chunk(c) for c in range(5)]
+        for c in range(PRELOAD):
+            load_next_chunk()
 
-        xw = x_raw[:].bitcast(F32)
-        x_banks = [
-            transpose_bank(xw, [a * 512 + g * 256 + u * P for u in range(2) for a in range(2)])
-            for g in range(2)
-        ]
-        xg = copy_units(x_banks, "sv")[0]
-        xq = quantise(const, xg, 2048, "x")
+        work = [("x", None), ("dv", 0), ("dv", 1)]
+        work.extend([("w", [h]) for h in range(2 * BY_HALVES)])
+        work.extend([("w", [2 * c, 2 * c + 1]) for c in range(BY_HALVES, N_CHUNKS)])
 
-        dvq = []
-        for d in range(2):
-            banks = t_weight(dv_raw[d], None)
-            dvq.append(cq(banks, "svsv"))
-        chunks.append(load_chunk(5))
-
-        halves = {}
-        pqs = []
-        for d in range(2):
-            p_acc = mx_p(dvq[d])
-            banks = t_weight(chunks[0][d][0], chunks[0][d][1])
-            pg = q_p(p_acc, d)
-            groups = copy_units(banks, "svsvsv")
-            pqs.append(quantise(const, pg, 1024, "p%d" % d))
-            halves[d] = [quantise(cod, g, 2048, "u") for g in groups]
-        chunks.append(load_chunk(6))
-
-        sil = {}
-        for h in range(N_HALVES):
-            c, d = divmod(h, 2)
-            accs = mx_half(halves[h], pqs[d])
-            for m in range(2):
-                if d == 0:
-                    s = epi.tile([P, 512], F32, tag="sil", name="sil")
-                    nc.scalar.activation(
-                        out=flat(s[:]),
-                        in_=natural(accs[m][:]),
-                        func=mybir.ActivationFunctionType.Silu,
-                    )
-                    sil[m] = s
-                else:
-                    o = epi.tile([P, 512], F32, tag="o", name="o")
-                    nc.vector.tensor_tensor(
-                        out=flat(o[:]),
-                        in0=natural(accs[m][:]),
-                        in1=flat(sil[m][:]),
-                        op=mybir.AluOpType.mult,
-                    )
-                    queue = nc.sync if c == N_CHUNKS - 1 else nc.gpsimd
-                    queue.dma_start(out=out_v[m][:, c * CHUNK : (c + 1) * CHUNK], in_=o[:])
-            nh = h + 2
-            if nh < N_HALVES:
-                wt, dt = chunks[nh // 2][nh % 2]
-                banks = t_weight(wt, dt)
-                halves[nh] = cq(banks, COPY_EVEN if nh % 2 == 0 else COPY_ODD)
+        units = None
+        for i in range(len(work) + 1):
+            banks = None
+            if i < len(work):
+                banks = transpose(work[i])
+                kind, arg = work[i]
+                if (kind == "dv" and arg == 1) or (kind == "w" and arg[-1] % 2 == 1):
+                    load_next_chunk()
+            accs = None
+            if i > 0:
+                accs = multiply(work[i - 1], units)
+            if i < len(work):
+                units = quantise_item(work[i], banks)
+            if i > 0:
+                finish(work[i - 1], accs)

@@ -102,14 +102,14 @@ def tile_merge_mixtralsparsemoeblock_pa_kernel(
             else:
                 nc.scalar.copy(out=dst, in_=src)
 
-        def regroup(banks, vector_helps):
+        def regroup(banks, helped):
             groups = []
             for i in range(len(banks) // 2):
                 g = grp.tile([P, 2048], BF16, tag="g", name="g", align_bytes=64)
                 gw = g[:].bitcast(F32)
                 for b in range(2):
                     copy_out(
-                        vector_helps and b == 1,
+                        b == 1 and i < helped,
                         gw[:, b * BANK : (b + 1) * BANK].rearrange("q (n u) -> q n u", u=2),
                         banks[2 * i + b][:].rearrange("q (u n) -> q n u", u=2),
                     )
@@ -156,14 +156,14 @@ def tile_merge_mixtralsparsemoeblock_pa_kernel(
         def quantise_item(item, banks):
             kind, arg = item
             if kind == "x":
-                small["x"] = quantise(const, regroup(banks, True)[0], 2048, "x")
+                small["x"] = quantise(const, regroup(banks, 1)[0], 2048, "x")
                 return None
             if kind == "dv":
-                groups = regroup(banks, True)
+                groups = regroup(banks, 2)
             else:
                 groups = []
                 for i, h in enumerate(arg):
-                    groups.extend(regroup(banks[6 * i : 6 * i + 6], h % 2 == 0))
+                    groups.extend(regroup(banks[6 * i : 6 * i + 6], 1 + h % 2))
             return [quantise(cod, g, 2048, "u") for g in groups]
 
         def multiply(item, units):

@@ -16,7 +16,6 @@ BANK = 512
 N_BANKS = 8
 CHUNK = 512
 N_CHUNKS = I // CHUNK
-BY_HALVES = 7
 PRELOAD = 3
 
 FLOPS = 2 * T * (2 * H * I + 2 * H * R + 2 * R * I)
@@ -29,8 +28,8 @@ def tile_merge_mixtralsparsemoeblock_pa_kernel(
     with ExitStack() as ctx:
         const = ctx.enter_context(tc.tile_pool(name="const", bufs=1))
         raw = ctx.enter_context(tc.tile_pool(name="raw", bufs=2 * PRELOAD + 2))
-        grp = ctx.enter_context(tc.tile_pool(name="grp", bufs=8))
-        cod = ctx.enter_context(tc.tile_pool(name="cod", bufs=14))
+        grp = ctx.enter_context(tc.tile_pool(name="grp", bufs=3))
+        cod = ctx.enter_context(tc.tile_pool(name="cod", bufs=4))
         act = ctx.enter_context(tc.tile_pool(name="act", bufs=4))
         res = ctx.enter_context(tc.tile_pool(name="res", bufs=2 * N_CHUNKS))
         psum = ctx.enter_context(tc.psum_pool(name="psum", bufs=1))
@@ -42,15 +41,13 @@ def tile_merge_mixtralsparsemoeblock_pa_kernel(
         nc.vector.memset(warm[:], 0.0)
         nc.scalar.activation(out=warm[:, 4:8], in_=warm[:, 0:4], func=SILU)
 
-        out_v = out.rearrange("(p j) i -> j p i", j=2)
-
-        def load(tag, width, src):
-            t = raw.tile([P, width], BF16, tag=tag, name=tag)
-            nc.sync.dma_start(out=t[:], in_=src)
+        def load_rows(tag, src, j):
+            t = raw.tile([P, j * src.shape[1]], BF16, tag=tag, name=tag)
+            nc.sync.dma_start(out=t[:], in_=src.rearrange("(p j) k -> p (j k)", j=j))
             return t
 
         def load_dv(dv):
-            t = raw.tile([P, 4096], BF16, tag="w", name="w")
+            t = raw.tile([P, 4 * H], BF16, tag="w", name="w")
             nc.sync.dma_start(
                 out=t[:].rearrange("p (u f) -> p u f", u=2),
                 in_=dv.rearrange("(u p e) k -> p u (e k)", u=2, e=2),
@@ -61,14 +58,13 @@ def tile_merge_mixtralsparsemoeblock_pa_kernel(
 
         def load_next_chunk():
             c = len(chunks)
-            if c == N_CHUNKS:
-                return
-            rows = slice(c * CHUNK, (c + 1) * CHUNK)
-            w1 = load("w", 4096, Wmean1[rows, :].rearrange("(p j) k -> p (j k)", j=4))
-            d1 = load("d", 2048, du1[rows, :].rearrange("(p j) k -> p (j k)", j=4))
-            w3 = load("w", 4096, Wmean3[rows, :].rearrange("(p j) k -> p (j k)", j=4))
-            d3 = load("d", 2048, du3[rows, :].rearrange("(p j) k -> p (j k)", j=4))
-            chunks.append([(w1, d1), (w3, d3)])
+            if c < N_CHUNKS:
+                rows = slice(c * CHUNK, (c + 1) * CHUNK)
+                w1 = load_rows("w", Wmean1[rows, :], 4)
+                d1 = load_rows("d", du1[rows, :], 4)
+                w3 = load_rows("w", Wmean3[rows, :], 4)
+                d3 = load_rows("d", du3[rows, :], 4)
+                chunks.append([(w1, d1), (w3, d3)])
 
         ring = [0]
 
@@ -77,7 +73,9 @@ def tile_merge_mixtralsparsemoeblock_pa_kernel(
             ring[0] = ring[0] + 1
             return psum.tile([P, BANK], F32, tag="bank%d" % k, name="bank%d" % k)
 
-        def transpose_bank(words, first, stride, k0):
+        def transpose_bank(tile, n_groups, first, k0):
+            words = tile[:].bitcast(F32)
+            stride = words.shape[1] // n_groups
             bank = next_bank()
             for u in range(2):
                 for a in range(2):
@@ -87,13 +85,9 @@ def tile_merge_mixtralsparsemoeblock_pa_kernel(
             return bank
 
         def transpose_weight(wt, dt):
-            banks = []
-            for g in range(2):
-                for b in range(2):
-                    banks.append(transpose_bank(wt[:].bitcast(F32), 2 * b, 512, 256 * g))
+            banks = [transpose_bank(wt, 4, 2 * b, 256 * g) for g in range(2) for b in range(2)]
             if dt is not None:
-                for b in range(2):
-                    banks.append(transpose_bank(dt[:].bitcast(F32), 2 * b, 256, 0))
+                banks.extend([transpose_bank(dt, 4, 2 * b, 0) for b in range(2)])
             return banks
 
         def copy_out(on_vector, dst, src):
@@ -102,23 +96,27 @@ def tile_merge_mixtralsparsemoeblock_pa_kernel(
             else:
                 nc.scalar.copy(out=dst, in_=src)
 
-        def regroup(banks, helped):
-            groups = []
-            for i in range(len(banks) // 2):
-                g = grp.tile([P, 2048], BF16, tag="g", name="g", align_bytes=64)
-                gw = g[:].bitcast(F32)
-                for b in range(2):
-                    copy_out(
-                        b == 1 and i < helped,
-                        gw[:, b * BANK : (b + 1) * BANK].rearrange("q (n u) -> q n u", u=2),
-                        banks[2 * i + b][:].rearrange("q (u n) -> q n u", u=2),
-                    )
-                groups.append(g)
-            return groups
+        def vector_share(n_banks, helped):
+            return [b % 2 == 1 and b // 2 < helped for b in range(n_banks)]
 
-        def quantise(pool, g, width, tag):
-            c = pool.tile([P, width // 4], U32, tag="c" + tag, name="c" + tag, align_bytes=64)
-            s = pool.tile([P, width // 4], U8, tag="s" + tag, name="s" + tag, align_bytes=64)
+        def regroup(banks, on_vector):
+            g = grp.tile(
+                [P, 2 * BANK * len(banks)], BF16,
+                tag="g%d" % len(banks), name="g%d" % len(banks), align_bytes=64,
+            )
+            words = g[:].bitcast(F32)
+            for b, bank in enumerate(banks):
+                copy_out(
+                    on_vector[b],
+                    words[:, b * BANK : (b + 1) * BANK].rearrange("q (n u) -> q n u", u=2),
+                    bank[:].rearrange("q (u n) -> q n u", u=2),
+                )
+            return g
+
+        def quantise(pool, g, tag):
+            width = g.shape[1] // 4
+            c = pool.tile([P, width], U32, tag="c" + tag, name="c" + tag, align_bytes=64)
+            s = pool.tile([P, width], U8, tag="s" + tag, name="s" + tag, align_bytes=64)
             nc.vector.quantize_mx(out=c[:].bitcast(FP8X4), scales=s[:], in_=g[:])
             return (c, s)
 
@@ -133,111 +131,107 @@ def tile_merge_mixtralsparsemoeblock_pa_kernel(
                 stop=stop,
             )
 
-        def natural(ap):
-            return ap.rearrange("t (j p) -> t p j", j=4)
+        def by_row(acc):
+            return acc.rearrange("t (j p) -> t p j", j=4)
 
-        def flat(ap):
-            return ap.rearrange("t (p j) -> t p j", j=4)
+        def as_rows(tile):
+            return tile.rearrange("t (p j) -> t p j", j=4)
 
-        small = {}
+        out_tiles = out.rearrange("(p m) i -> m p i", m=2)
+
+        quantised = {}
         silu_of = {}
 
-        def transpose(item):
-            kind, arg = item
+        def transpose(kind, n):
             if kind == "x":
-                return [transpose_bank(x_raw[:].bitcast(F32), 0, 512, 256 * g) for g in range(2)]
+                return [transpose_bank(x_raw, 2, 0, 256 * g) for g in range(2)]
             if kind == "dv":
-                return transpose_weight(dv_raw[arg], None)
-            banks = []
-            for h in arg:
-                banks.extend(transpose_weight(chunks[h // 2][h % 2][0], chunks[h // 2][h % 2][1]))
-            return banks
+                return transpose_weight(dv_raw[n], None)
+            return transpose_weight(chunks[n // 2][n % 2][0], chunks[n // 2][n % 2][1])
 
-        def quantise_item(item, banks):
-            kind, arg = item
+        def regroup_and_quantise(kind, n, banks):
             if kind == "x":
-                small["x"] = quantise(const, regroup(banks, 1)[0], 2048, "x")
+                quantised["x"] = quantise(const, regroup(banks, vector_share(2, 1)), "x")
                 return None
             if kind == "dv":
-                groups = regroup(banks, 2)
-            else:
-                groups = []
-                for i, h in enumerate(arg):
-                    groups.extend(regroup(banks[6 * i : 6 * i + 6], 1 + h % 2))
-            return [quantise(cod, g, 2048, "u") for g in groups]
+                q = quantise(cod, regroup(banks, vector_share(4, 2)), "4")
+                return [(q, 0), (q, BANK)]
+            share = vector_share(6, 2 - n % 2)
+            gw = regroup(banks[0:4], share[0:4])
+            gd = regroup(banks[4:6], share[4:6])
+            qw = quantise(cod, gw, "4")
+            qd = quantise(cod, gd, "2")
+            return [(qw, 0), (qw, BANK), (qd, 0)]
 
-        def multiply(item, units):
-            kind, arg = item
+        def multiply(kind, n, operands):
             accs = []
             if kind == "dv":
                 for m in range(2):
                     acc = next_bank()
                     for t in range(4):
                         for g in range(2):
-                            mx(acc[:, t * P : (t + 1) * P], units[g], t * P,
-                               small["x"], 256 * g + m * P, P, g == 0, g == 1)
+                            q, first = operands[g]
+                            mx(acc[:, t * P : (t + 1) * P], q, first + t * P,
+                               quantised["x"], 256 * g + m * P, P, g == 0, g == 1)
                     accs.append(acc)
-            if kind == "w":
-                for i, h in enumerate(arg):
-                    for m in range(2):
-                        acc = next_bank()
-                        mx(acc[:], small["x"], m * P, units[3 * i], 0, BANK, True, False)
-                        mx(acc[:], small["x"], 256 + m * P, units[3 * i + 1], 0, BANK, False, False)
-                        mx(acc[:], small[h % 2], m * P, units[3 * i + 2], 0, BANK, False, True)
-                        accs.append(acc)
+            if kind == "half":
+                for m in range(2):
+                    acc = next_bank()
+                    for g in range(2):
+                        q, first = operands[g]
+                        mx(acc[:], quantised["x"], 256 * g + m * P, q, first, BANK, g == 0, False)
+                    q, first = operands[2]
+                    mx(acc[:], quantised[n % 2], m * P, q, first, BANK, False, True)
+                    accs.append(acc)
             return accs
 
-        def finish(item, accs):
-            kind, arg = item
+        def finish(kind, n, accs):
             if kind == "dv":
-                pg = const.tile([P, 1024], BF16, name="pg%d" % arg, align_bytes=64)
+                pg = const.tile([P, 4 * T], BF16, name="pg%d" % n, align_bytes=64)
                 for m in range(2):
                     copy_out(
                         m == 0,
-                        pg[:, m * 512 : (m + 1) * 512].rearrange("q (n t) -> q n t", t=4),
+                        pg[:, m * BANK : (m + 1) * BANK].rearrange("q (n t) -> q n t", t=4),
                         accs[m][:].rearrange("q (t n) -> q n t", t=4),
                     )
-                small[arg] = quantise(const, pg, 1024, "p%d" % arg)
-            if kind == "w":
-                for i, h in enumerate(arg):
-                    for m in range(2):
-                        acc = accs[2 * i + m]
-                        if h % 2 == 0:
-                            s = act.tile([P, CHUNK], F32, tag="silu", name="silu")
-                            nc.scalar.activation(out=flat(s[:]), in_=natural(acc[:]), func=SILU)
-                            silu_of[m] = s
-                        else:
-                            c = h // 2
-                            o = res.tile([P, CHUNK], F32, tag="o", name="o")
-                            nc.vector.tensor_tensor(
-                                out=flat(o[:]),
-                                in0=natural(acc[:]),
-                                in1=flat(silu_of[m][:]),
-                                op=mybir.AluOpType.mult,
-                            )
-                            nc.sync.dma_start(out=out_v[m][:, c * CHUNK : (c + 1) * CHUNK], in_=o[:])
+                quantised[n] = quantise(const, pg, "p%d" % n)
+            if kind == "half":
+                c = n // 2
+                for m in range(2):
+                    if n % 2 == 0:
+                        s = act.tile([P, CHUNK], F32, tag="silu", name="silu")
+                        nc.scalar.activation(out=as_rows(s[:]), in_=by_row(accs[m][:]), func=SILU)
+                        silu_of[m] = s
+                    else:
+                        o = res.tile([P, CHUNK], F32, tag="o", name="o")
+                        nc.vector.tensor_tensor(
+                            out=as_rows(o[:]),
+                            in0=by_row(accs[m][:]),
+                            in1=as_rows(silu_of[m][:]),
+                            op=mybir.AluOpType.mult,
+                        )
+                        nc.sync.dma_start(out=out_tiles[m][:, c * CHUNK : (c + 1) * CHUNK], in_=o[:])
 
-        x_raw = load("d", 2048, x.rearrange("(p j) k -> p (j k)", j=2))
+        x_raw = load_rows("d", x, 2)
         dv_raw = [load_dv(dv1), load_dv(dv3)]
         for c in range(PRELOAD):
             load_next_chunk()
 
-        work = [("x", None), ("dv", 0), ("dv", 1)]
-        work.extend([("w", [h]) for h in range(2 * BY_HALVES)])
-        work.extend([("w", [2 * c, 2 * c + 1]) for c in range(BY_HALVES, N_CHUNKS)])
+        work = [("x", 0), ("dv", 0), ("dv", 1)]
+        work.extend([("half", h) for h in range(2 * N_CHUNKS)])
 
-        units = None
+        operands = None
         for i in range(len(work) + 1):
             banks = None
             if i < len(work):
-                banks = transpose(work[i])
-                kind, arg = work[i]
-                if (kind == "dv" and arg == 1) or (kind == "w" and arg[-1] % 2 == 1):
+                kind, n = work[i]
+                banks = transpose(kind, n)
+                if kind != "x" and n % 2 == 1:
                     load_next_chunk()
             accs = None
             if i > 0:
-                accs = multiply(work[i - 1], units)
+                accs = multiply(work[i - 1][0], work[i - 1][1], operands)
             if i < len(work):
-                units = quantise_item(work[i], banks)
+                operands = regroup_and_quantise(work[i][0], work[i][1], banks)
             if i > 0:
-                finish(work[i - 1], accs)
+                finish(work[i - 1][0], work[i - 1][1], accs)

@@ -28,8 +28,8 @@ def tile_merge_mixtralsparsemoeblock_pa_kernel(
     with ExitStack() as ctx:
         const = ctx.enter_context(tc.tile_pool(name="const", bufs=1))
         raw = ctx.enter_context(tc.tile_pool(name="raw", bufs=2 * PRELOAD + 2))
-        grp = ctx.enter_context(tc.tile_pool(name="grp", bufs=3))
-        cod = ctx.enter_context(tc.tile_pool(name="cod", bufs=4))
+        grp = ctx.enter_context(tc.tile_pool(name="grp", bufs=8))
+        cod = ctx.enter_context(tc.tile_pool(name="cod", bufs=14))
         act = ctx.enter_context(tc.tile_pool(name="act", bufs=4))
         res = ctx.enter_context(tc.tile_pool(name="res", bufs=2 * N_CHUNKS))
         psum = ctx.enter_context(tc.psum_pool(name="psum", bufs=1))
@@ -41,18 +41,18 @@ def tile_merge_mixtralsparsemoeblock_pa_kernel(
         nc.vector.memset(warm[:], 0.0)
         nc.scalar.activation(out=warm[:, 4:8], in_=warm[:, 0:4], func=SILU)
 
-        def load_rows(tag, src, j):
-            t = raw.tile([P, j * src.shape[1]], BF16, tag=tag, name=tag)
-            nc.sync.dma_start(out=t[:], in_=src.rearrange("(p j) k -> p (j k)", j=j))
-            return t
+        def load_rows(tag, src, rows_each):
+            tile = raw.tile([P, rows_each * src.shape[1]], BF16, tag=tag, name=tag)
+            nc.sync.dma_start(out=tile[:], in_=src.rearrange("(p j) k -> p (j k)", j=rows_each))
+            return tile
 
         def load_dv(dv):
-            t = raw.tile([P, 4 * H], BF16, tag="w", name="w")
+            tile = raw.tile([P, 4 * H], BF16, tag="w", name="w")
             nc.sync.dma_start(
-                out=t[:].rearrange("p (u f) -> p u f", u=2),
+                out=tile[:].rearrange("p (u f) -> p u f", u=2),
                 in_=dv.rearrange("(u p e) k -> p u (e k)", u=2, e=2),
             )
-            return t
+            return tile
 
         chunks = []
 
@@ -73,21 +73,21 @@ def tile_merge_mixtralsparsemoeblock_pa_kernel(
             ring[0] = ring[0] + 1
             return psum.tile([P, BANK], F32, tag="bank%d" % k, name="bank%d" % k)
 
-        def transpose_bank(tile, n_groups, first, k0):
+        def transpose_bank(tile, n_groups, group0, word0):
             words = tile[:].bitcast(F32)
             stride = words.shape[1] // n_groups
             bank = next_bank()
             for u in range(2):
                 for a in range(2):
-                    src = (first + a) * stride + k0 + u * P
+                    src = (group0 + a) * stride + word0 + u * P
                     pos = (2 * u + a) * P
                     nc.tensor.transpose(bank[:, pos : pos + P], words[:, src : src + P], ident[:])
             return bank
 
-        def transpose_weight(wt, dt):
-            banks = [transpose_bank(wt, 4, 2 * b, 256 * g) for g in range(2) for b in range(2)]
-            if dt is not None:
-                banks.extend([transpose_bank(dt, 4, 2 * b, 0) for b in range(2)])
+        def transpose_weight(weight, delta):
+            banks = [transpose_bank(weight, 4, 2 * b, 256 * g) for g in range(2) for b in range(2)]
+            if delta is not None:
+                banks.extend([transpose_bank(delta, 4, 2 * b, 0) for b in range(2)])
             return banks
 
         def copy_out(on_vector, dst, src):
@@ -96,37 +96,34 @@ def tile_merge_mixtralsparsemoeblock_pa_kernel(
             else:
                 nc.scalar.copy(out=dst, in_=src)
 
-        def vector_share(n_banks, helped):
-            return [b % 2 == 1 and b // 2 < helped for b in range(n_banks)]
+        def regroup(banks, helped):
+            grouped = []
+            for i in range(len(banks) // 2):
+                tile = grp.tile([P, 4 * BANK], BF16, tag="g", name="g", align_bytes=64)
+                words = tile[:].bitcast(F32)
+                for b in range(2):
+                    copy_out(
+                        b == 1 and i < helped,
+                        words[:, b * BANK : (b + 1) * BANK].rearrange("q (n u) -> q n u", u=2),
+                        banks[2 * i + b][:].rearrange("q (u n) -> q n u", u=2),
+                    )
+                grouped.append(tile)
+            return grouped
 
-        def regroup(banks, on_vector):
-            g = grp.tile(
-                [P, 2 * BANK * len(banks)], BF16,
-                tag="g%d" % len(banks), name="g%d" % len(banks), align_bytes=64,
-            )
-            words = g[:].bitcast(F32)
-            for b, bank in enumerate(banks):
-                copy_out(
-                    on_vector[b],
-                    words[:, b * BANK : (b + 1) * BANK].rearrange("q (n u) -> q n u", u=2),
-                    bank[:].rearrange("q (u n) -> q n u", u=2),
-                )
-            return g
+        def quantise(pool, tile, tag):
+            width = tile.shape[1] // 4
+            codes = pool.tile([P, width], U32, tag="c" + tag, name="c" + tag, align_bytes=64)
+            scales = pool.tile([P, width], U8, tag="s" + tag, name="s" + tag, align_bytes=64)
+            nc.vector.quantize_mx(out=codes[:].bitcast(FP8X4), scales=scales[:], in_=tile[:])
+            return (codes, scales)
 
-        def quantise(pool, g, tag):
-            width = g.shape[1] // 4
-            c = pool.tile([P, width], U32, tag="c" + tag, name="c" + tag, align_bytes=64)
-            s = pool.tile([P, width], U8, tag="s" + tag, name="s" + tag, align_bytes=64)
-            nc.vector.quantize_mx(out=c[:].bitcast(FP8X4), scales=s[:], in_=g[:])
-            return (c, s)
-
-        def mx(acc, lhs, l0, rhs, r0, n, start, stop):
+        def mx(acc, still, still0, moving, moving0, width, start, stop):
             nc.tensor.matmul_mx(
                 out=acc,
-                lhsT=lhs[0][:, l0 : l0 + P].bitcast(FP8X4),
-                lhsT_scale=lhs[1][:, l0 : l0 + P],
-                rhs=rhs[0][:, r0 : r0 + n].bitcast(FP8X4),
-                rhs_scale=rhs[1][:, r0 : r0 + n],
+                lhsT=still[0][:, still0 : still0 + P].bitcast(FP8X4),
+                lhsT_scale=still[1][:, still0 : still0 + P],
+                rhs=moving[0][:, moving0 : moving0 + width].bitcast(FP8X4),
+                rhs_scale=moving[1][:, moving0 : moving0 + width],
                 start=start,
                 stop=stop,
             )
@@ -140,6 +137,7 @@ def tile_merge_mixtralsparsemoeblock_pa_kernel(
         out_tiles = out.rearrange("(p m) i -> m p i", m=2)
 
         quantised = {}
+        rounded = {}
         silu_of = {}
 
         def transpose(kind, n):
@@ -149,68 +147,59 @@ def tile_merge_mixtralsparsemoeblock_pa_kernel(
                 return transpose_weight(dv_raw[n], None)
             return transpose_weight(chunks[n // 2][n % 2][0], chunks[n // 2][n % 2][1])
 
-        def regroup_and_quantise(kind, n, banks):
+        def copy_share(kind, n):
+            return 1 + n % 2 if kind == "half" else 2
+
+        def quantise_operands(kind, grouped):
             if kind == "x":
-                quantised["x"] = quantise(const, regroup(banks, vector_share(2, 1)), "x")
-                return None
-            if kind == "dv":
-                q = quantise(cod, regroup(banks, vector_share(4, 2)), "4")
-                return [(q, 0), (q, BANK)]
-            share = vector_share(6, 2 - n % 2)
-            gw = regroup(banks[0:4], share[0:4])
-            gd = regroup(banks[4:6], share[4:6])
-            qw = quantise(cod, gw, "4")
-            qd = quantise(cod, gd, "2")
-            return [(qw, 0), (qw, BANK), (qd, 0)]
+                return [quantise(const, tile, "x") for tile in grouped]
+            return [quantise(cod, tile, "u") for tile in grouped]
 
         def multiply(kind, n, operands):
+            if kind == "x":
+                quantised["x"] = operands[0]
             accs = []
-            if kind == "dv":
-                for m in range(2):
+            for m in range(2):
+                if kind == "dv":
                     acc = next_bank()
                     for t in range(4):
                         for g in range(2):
-                            q, first = operands[g]
-                            mx(acc[:, t * P : (t + 1) * P], q, first + t * P,
+                            mx(acc[:, t * P : (t + 1) * P], operands[g], t * P,
                                quantised["x"], 256 * g + m * P, P, g == 0, g == 1)
                     accs.append(acc)
-            if kind == "half":
-                for m in range(2):
+                if kind == "half":
                     acc = next_bank()
-                    for g in range(2):
-                        q, first = operands[g]
-                        mx(acc[:], quantised["x"], 256 * g + m * P, q, first, BANK, g == 0, False)
-                    q, first = operands[2]
-                    mx(acc[:], quantised[n % 2], m * P, q, first, BANK, False, True)
+                    mx(acc[:], quantised["x"], m * P, operands[0], 0, BANK, True, False)
+                    mx(acc[:], quantised["x"], 256 + m * P, operands[1], 0, BANK, False, False)
+                    mx(acc[:], quantised[n % 2], m * P, operands[2], 0, BANK, False, True)
                     accs.append(acc)
             return accs
 
-        def finish(kind, n, accs):
+        def finish(kind, n, accs, m):
             if kind == "dv":
-                pg = const.tile([P, 4 * T], BF16, name="pg%d" % n, align_bytes=64)
-                for m in range(2):
-                    copy_out(
-                        m == 0,
-                        pg[:, m * BANK : (m + 1) * BANK].rearrange("q (n t) -> q n t", t=4),
-                        accs[m][:].rearrange("q (t n) -> q n t", t=4),
-                    )
-                quantised[n] = quantise(const, pg, "p%d" % n)
-            if kind == "half":
+                if m == 0:
+                    rounded[n] = const.tile([P, 4 * T], BF16, name="pg%d" % n, align_bytes=64)
+                copy_out(
+                    m == 0,
+                    rounded[n][:, m * BANK : (m + 1) * BANK].rearrange("q (n t) -> q n t", t=4),
+                    accs[m][:].rearrange("q (t n) -> q n t", t=4),
+                )
+                if m == 1:
+                    quantised[n] = quantise(const, rounded[n], "p%d" % n)
+            if kind == "half" and n % 2 == 0:
+                gated = act.tile([P, CHUNK], F32, tag="silu", name="silu")
+                nc.scalar.activation(out=as_rows(gated[:]), in_=by_row(accs[m][:]), func=SILU)
+                silu_of[m] = gated
+            if kind == "half" and n % 2 == 1:
                 c = n // 2
-                for m in range(2):
-                    if n % 2 == 0:
-                        s = act.tile([P, CHUNK], F32, tag="silu", name="silu")
-                        nc.scalar.activation(out=as_rows(s[:]), in_=by_row(accs[m][:]), func=SILU)
-                        silu_of[m] = s
-                    else:
-                        o = res.tile([P, CHUNK], F32, tag="o", name="o")
-                        nc.vector.tensor_tensor(
-                            out=as_rows(o[:]),
-                            in0=by_row(accs[m][:]),
-                            in1=as_rows(silu_of[m][:]),
-                            op=mybir.AluOpType.mult,
-                        )
-                        nc.sync.dma_start(out=out_tiles[m][:, c * CHUNK : (c + 1) * CHUNK], in_=o[:])
+                z = res.tile([P, CHUNK], F32, tag="o", name="o")
+                nc.vector.tensor_tensor(
+                    out=as_rows(z[:]),
+                    in0=by_row(accs[m][:]),
+                    in1=as_rows(silu_of[m][:]),
+                    op=mybir.AluOpType.mult,
+                )
+                nc.sync.dma_start(out=out_tiles[m][:, c * CHUNK : (c + 1) * CHUNK], in_=z[:])
 
         x_raw = load_rows("d", x, 2)
         dv_raw = [load_dv(dv1), load_dv(dv3)]
@@ -219,19 +208,20 @@ def tile_merge_mixtralsparsemoeblock_pa_kernel(
 
         work = [("x", 0), ("dv", 0), ("dv", 1)]
         work.extend([("half", h) for h in range(2 * N_CHUNKS)])
+        work.append(("end", 0))
 
-        operands = None
-        for i in range(len(work) + 1):
-            banks = None
-            if i < len(work):
-                kind, n = work[i]
+        before = ("start", 0)
+        operands = []
+        for kind, n in work:
+            banks = []
+            if kind != "end":
                 banks = transpose(kind, n)
-                if kind != "x" and n % 2 == 1:
-                    load_next_chunk()
-            accs = None
-            if i > 0:
-                accs = multiply(work[i - 1][0], work[i - 1][1], operands)
-            if i < len(work):
-                operands = regroup_and_quantise(work[i][0], work[i][1], banks)
-            if i > 0:
-                finish(work[i - 1][0], work[i - 1][1], accs)
+            if kind in ("dv", "half") and n % 2 == 1:
+                load_next_chunk()
+            accs = multiply(before[0], before[1], operands)
+            grouped = regroup(banks, copy_share(kind, n))
+            operands = quantise_operands(kind, grouped[0:2])
+            finish(before[0], before[1], accs, 0)
+            operands.extend(quantise_operands(kind, grouped[2:3]))
+            finish(before[0], before[1], accs, 1)
+            before = (kind, n)

from contextlib import ExitStack

import concourse.mybir as mybir
from concourse.masks import make_identity

BF16 = mybir.dt.bfloat16
F32 = mybir.dt.float32
U32 = mybir.dt.uint32
U8 = mybir.dt.uint8
FP8X4 = mybir.dt.float8_e4m3fn_x4
SILU = mybir.ActivationFunctionType.Silu

T, H, I, R = 256, 1024, 3584, 512
P = 128
BANK = 512
N_BANKS = 8
CHUNK = 512
N_CHUNKS = I // CHUNK
PRELOAD = 3

FLOPS = 2 * T * (2 * H * I + 2 * H * R + 2 * R * I)


def tile_merge_mixtralsparsemoeblock_pa_kernel(
    tc, x, Wmean1, Wmean3, du1, dv1, du3, dv3, out
):
    nc = tc.nc
    with ExitStack() as ctx:
        const = ctx.enter_context(tc.tile_pool(name="const", bufs=1))
        raw = ctx.enter_context(tc.tile_pool(name="raw", bufs=2 * PRELOAD + 2))
        grp = ctx.enter_context(tc.tile_pool(name="grp", bufs=8))
        cod = ctx.enter_context(tc.tile_pool(name="cod", bufs=14))
        act = ctx.enter_context(tc.tile_pool(name="act", bufs=4))
        res = ctx.enter_context(tc.tile_pool(name="res", bufs=2 * N_CHUNKS))
        psum = ctx.enter_context(tc.psum_pool(name="psum", bufs=1))
        ctx.enter_context(tc.manual_schedule())

        ident = const.tile([P, P], F32, name="ident")
        make_identity(nc, ident[:])
        warm = const.tile([P, 8], F32, name="warm")
        nc.vector.memset(warm[:], 0.0)
        nc.scalar.activation(out=warm[:, 4:8], in_=warm[:, 0:4], func=SILU)

        def load_rows(tag, src, rows_each):
            tile = raw.tile([P, rows_each * src.shape[1]], BF16, tag=tag, name=tag)
            nc.sync.dma_start(out=tile[:], in_=src.rearrange("(p j) k -> p (j k)", j=rows_each))
            return tile

        def load_dv(dv):
            tile = raw.tile([P, 4 * H], BF16, tag="w", name="w")
            nc.sync.dma_start(
                out=tile[:].rearrange("p (u f) -> p u f", u=2),
                in_=dv.rearrange("(u p e) k -> p u (e k)", u=2, e=2),
            )
            return tile

        chunks = []

        def load_next_chunk():
            c = len(chunks)
            if c < N_CHUNKS:
                rows = slice(c * CHUNK, (c + 1) * CHUNK)
                w1 = load_rows("w", Wmean1[rows, :], 4)
                d1 = load_rows("d", du1[rows, :], 4)
                w3 = load_rows("w", Wmean3[rows, :], 4)
                d3 = load_rows("d", du3[rows, :], 4)
                chunks.append([(w1, d1), (w3, d3)])

        ring = [0]

        def next_bank():
            k = ring[0] % N_BANKS
            ring[0] = ring[0] + 1
            return psum.tile([P, BANK], F32, tag="bank%d" % k, name="bank%d" % k)

        def transpose_bank(tile, n_groups, group0, word0):
            words = tile[:].bitcast(F32)
            stride = words.shape[1] // n_groups
            bank = next_bank()
            for u in range(2):
                for a in range(2):
                    src = (group0 + a) * stride + word0 + u * P
                    pos = (2 * u + a) * P
                    nc.tensor.transpose(bank[:, pos : pos + P], words[:, src : src + P], ident[:])
            return bank

        def transpose_weight(weight, delta):
            banks = [transpose_bank(weight, 4, 2 * b, 256 * g) for g in range(2) for b in range(2)]
            if delta is not None:
                banks.extend([transpose_bank(delta, 4, 2 * b, 0) for b in range(2)])
            return banks

        def copy_out(on_vector, dst, src):
            if on_vector:
                nc.vector.tensor_copy(out=dst, in_=src)
            else:
                nc.scalar.copy(out=dst, in_=src)

        def regroup(banks, helped):
            grouped = []
            for i in range(len(banks) // 2):
                tile = grp.tile([P, 4 * BANK], BF16, tag="g", name="g", align_bytes=64)
                words = tile[:].bitcast(F32)
                for b in range(2):
                    copy_out(
                        b == 1 and i < helped,
                        words[:, b * BANK : (b + 1) * BANK].rearrange("q (n u) -> q n u", u=2),
                        banks[2 * i + b][:].rearrange("q (u n) -> q n u", u=2),
                    )
                grouped.append(tile)
            return grouped

        def quantise(pool, tile, tag):
            width = tile.shape[1] // 4
            codes = pool.tile([P, width], U32, tag="c" + tag, name="c" + tag, align_bytes=64)
            scales = pool.tile([P, width], U8, tag="s" + tag, name="s" + tag, align_bytes=64)
            nc.vector.quantize_mx(out=codes[:].bitcast(FP8X4), scales=scales[:], in_=tile[:])
            return (codes, scales)

        def mx(acc, still, still0, moving, moving0, width, start, stop):
            nc.tensor.matmul_mx(
                out=acc,
                lhsT=still[0][:, still0 : still0 + P].bitcast(FP8X4),
                lhsT_scale=still[1][:, still0 : still0 + P],
                rhs=moving[0][:, moving0 : moving0 + width].bitcast(FP8X4),
                rhs_scale=moving[1][:, moving0 : moving0 + width],
                start=start,
                stop=stop,
            )

        def by_row(acc):
            return acc.rearrange("t (j p) -> t p j", j=4)

        def as_rows(tile):
            return tile.rearrange("t (p j) -> t p j", j=4)

        out_tiles = out.rearrange("(p m) i -> m p i", m=2)

        quantised = {}
        rounded = {}
        silu_of = {}

        def transpose(kind, n):
            if kind == "x":
                return [transpose_bank(x_raw, 2, 0, 256 * g) for g in range(2)]
            if kind == "dv":
                return transpose_weight(dv_raw[n], None)
            return transpose_weight(chunks[n // 2][n % 2][0], chunks[n // 2][n % 2][1])

        def copy_share(kind, n):
            return 1 + n % 2 if kind == "half" else 2

        def quantise_operands(kind, grouped):
            if kind == "x":
                return [quantise(const, tile, "x") for tile in grouped]
            return [quantise(cod, tile, "u") for tile in grouped]

        def multiply(kind, n, operands):
            if kind == "x":
                quantised["x"] = operands[0]
            accs = []
            for m in range(2):
                if kind == "dv":
                    acc = next_bank()
                    for t in range(4):
                        for g in range(2):
                            mx(acc[:, t * P : (t + 1) * P], operands[g], t * P,
                               quantised["x"], 256 * g + m * P, P, g == 0, g == 1)
                    accs.append(acc)
                if kind == "half":
                    acc = next_bank()
                    mx(acc[:], quantised["x"], m * P, operands[0], 0, BANK, True, False)
                    mx(acc[:], quantised["x"], 256 + m * P, operands[1], 0, BANK, False, False)
                    mx(acc[:], quantised[n % 2], m * P, operands[2], 0, BANK, False, True)
                    accs.append(acc)
            return accs

        def finish(kind, n, accs, m):
            if kind == "dv":
                if m == 0:
                    rounded[n] = const.tile([P, 4 * T], BF16, name="pg%d" % n, align_bytes=64)
                copy_out(
                    m == 0,
                    rounded[n][:, m * BANK : (m + 1) * BANK].rearrange("q (n t) -> q n t", t=4),
                    accs[m][:].rearrange("q (t n) -> q n t", t=4),
                )
                if m == 1:
                    quantised[n] = quantise(const, rounded[n], "p%d" % n)
            if kind == "half" and n % 2 == 0:
                gated = act.tile([P, CHUNK], F32, tag="silu", name="silu")
                nc.scalar.activation(out=as_rows(gated[:]), in_=by_row(accs[m][:]), func=SILU)
                silu_of[m] = gated
            if kind == "half" and n % 2 == 1:
                c = n // 2
                z = res.tile([P, CHUNK], F32, tag="o", name="o")
                nc.vector.tensor_tensor(
                    out=as_rows(z[:]),
                    in0=by_row(accs[m][:]),
                    in1=as_rows(silu_of[m][:]),
                    op=mybir.AluOpType.mult,
                )
                nc.sync.dma_start(out=out_tiles[m][:, c * CHUNK : (c + 1) * CHUNK], in_=z[:])

        x_raw = load_rows("d", x, 2)
        dv_raw = [load_dv(dv1), load_dv(dv3)]
        for c in range(PRELOAD):
            load_next_chunk()

        work = [("x", 0), ("dv", 0), ("dv", 1)]
        work.extend([("half", h) for h in range(2 * N_CHUNKS)])
        work.append(("end", 0))

        before = ("start", 0)
        operands = []
        for kind, n in work:
            banks = []
            if kind != "end":
                banks = transpose(kind, n)
            if kind in ("dv", "half") and n % 2 == 1:
                load_next_chunk()
            accs = multiply(before[0], before[1], operands)
            grouped = regroup(banks, copy_share(kind, n))
            operands = quantise_operands(kind, grouped[0:2])
            finish(before[0], before[1], accs, 0)
            operands.extend(quantise_operands(kind, grouped[2:3]))
            finish(before[0], before[1], accs, 1)
            before = (kind, n)
